import numpy as np
import ml_dtypes


def mxq(x, axis, fmt="e4m3"):
    dtype, down = {"e4m3": (ml_dtypes.float8_e4m3fn, 7), "e5m2": (ml_dtypes.float8_e5m2, 14)}[fmt]
    v = np.moveaxis(np.asarray(x, np.float32).astype(ml_dtypes.bfloat16).astype(np.float64), axis, -1)
    blocks = v.reshape(v.shape[:-1] + (-1, 32))
    amax = np.abs(blocks).max(-1, keepdims=True)
    byte = np.maximum(np.where(amax > 0, np.frexp(amax)[1] - 1 + 127, 0) - down, 1)
    scale = np.exp2(byte - 127.0)
    codes = (blocks / scale).astype(np.float32).astype(dtype).astype(np.float64)
    return np.moveaxis((codes * scale).reshape(v.shape), -1, axis)


WIDE = False


def mx_kscale(k):
    if not WIDE:
        return np.ones(k)
    levels = np.array([10, -10, 5, -5, 0])
    a = np.random.permutation(np.resize(levels, k // 512 * 4)).reshape(k // 512, 4)
    idx = np.arange(k)
    return np.exp2(a[idx // 512, idx % 128 // 32])


BF16 = ml_dtypes.bfloat16


def bf(x):
    return np.asarray(x, np.float32).astype(BF16)


def f64(x):
    return np.asarray(x).astype(np.float64)


B, N, D, H, DH = 2, 512, 1024, 8, 128
E = H * DH
K_POLY = 3
SIG = 2.0


def setup_inputs():
    s = mx_kscale(D)
    g = np.random.standard_normal
    lg = g((B, H, N, N)) * SIG
    e = np.exp(lg - lg.max(-1, keepdims=True))
    return {
        "x": bf(g((B, N, D)) * s),
        "att": bf(e / e.sum(-1, keepdims=True)),
        "Wv": bf(g((D, E)) * 1.5 / np.sqrt(D) / s[:, None]),
        "bv": bf(g(E) * 0.2),
        "w0": bf(0.25 + 0.05 * g(H)),
        "w1": bf(1.0 + 0.1 * g(H)),
        "wK": bf(0.2 + 0.03 * g(H)),
    }


def reference(x, att, Wv, bv, w0, w1, wK):
    v = (mxq(f64(x), 2, "e4m3") @ mxq(f64(Wv), 0, "e4m3")) + f64(bv)
    v = v.reshape(B, N, H, DH).transpose(0, 2, 1, 3)
    att = f64(att)
    att2 = mxq(att, 3, "e4m3") @ mxq(att, 2, "e4m3")
    attK = att + (K_POLY - 1) * (att2 - att)
    c0 = f64(w0)[None, :, None, None]
    c1 = f64(w1)[None, :, None, None]
    cK = f64(wK)[None, :, None, None]
    gf = c0 * np.eye(N)[None, None] + c1 * att + cK * attK
    out = mxq(gf, 3, "e4m3") @ mxq(v, 2, "e4m3")
    return out.transpose(0, 2, 1, 3).reshape(B, N, E)

@@ -1,0 +1,318 @@
+from contextlib import ExitStack
+
+import concourse.mybir as mybir
+from concourse.masks import make_identity
+
+BF16 = mybir.dt.bfloat16
+F32 = mybir.dt.float32
+U32 = mybir.dt.uint32
+U8 = mybir.dt.uint8
+FP8X4 = mybir.dt.float8_e4m3fn_x4
+MULT = mybir.AluOpType.mult
+ADD = mybir.AluOpType.add
+SUBTRACT = mybir.AluOpType.subtract
+COPY = mybir.ActivationFunctionType.Copy
+
+P = 128
+PACK = 4
+K_PASS = P * PACK
+B, N, D, H, DH = 2, 512, 1024, 8, 128
+HEADS = B * H
+D_PASSES = D // K_PASS
+UNIT = K_PASS * PACK
+SCALAR_TILES = 3
+DIAG_STEP = N + P
+
+FLOPS = 2 * B * N * D * D + HEADS * 2 * N * N * N + HEADS * 2 * N * N * DH
+
+ROWS = "(u q e) c -> q u e c"
+SLABS = "p (u e) c -> p u e c"
+
+
+def tile_gfsa_pa_kernel(tc, x, att, Wv, bv, w0, w1, wK, out):
+    nc = tc.nc
+    with ExitStack() as ctx:
+        resident = ctx.enter_context(tc.tile_pool(name="resident", bufs=1))
+        wide_pool = ctx.enter_context(tc.tile_pool(name="wide", bufs=2))
+        pair_pool = ctx.enter_context(tc.tile_pool(name="pair", bufs=3))
+        scaled_pool = ctx.enter_context(tc.tile_pool(name="scaled", bufs=3))
+        work_pool = ctx.enter_context(tc.tile_pool(name="work", bufs=2))
+        out_pool = ctx.enter_context(tc.tile_pool(name="outs", bufs=3))
+        tp_pool = ctx.enter_context(tc.psum_pool(name="tp", bufs=4))
+        mx_pool = ctx.enter_context(tc.psum_pool(name="mx", bufs=4))
+        ctx.enter_context(tc.manual_schedule())
+
+        ident = resident.tile([P, P], F32)
+        make_identity(nc, ident[:])
+
+        w0_bf = resident.tile([P, H], BF16)
+        w1_bf = resident.tile([P, H], BF16)
+        wk_bf = resident.tile([P, H], BF16)
+        nc.scalar.dma_start(out=w0_bf[:], in_=w0.partition_broadcast(P))
+        nc.scalar.dma_start(out=w1_bf[:], in_=w1.partition_broadcast(P))
+        nc.scalar.dma_start(out=wk_bf[:], in_=wK.partition_broadcast(P))
+
+        x_sb = [resident.tile([P, PACK, D], BF16, name="x_sb%d" % b) for b in range(B)]
+        w_sb = resident.tile([P, D_PASSES, PACK, D], BF16)
+        att_sb = [resident.tile([P, PACK, N], BF16, name="att_sb%d" % i) for i in range(HEADS)]
+        bias = resident.tile([P, D], BF16)
+
+        def load_att(i):
+            nc.sync.dma_start(
+                out=att_sb[i][:].rearrange(SLABS, u=2),
+                in_=att[i // H, i % H].rearrange(ROWS, u=2, e=2),
+            )
+
+        def load_x(b):
+            nc.sync.dma_start(out=x_sb[b][:].rearrange(SLABS, u=2), in_=x[b].rearrange(ROWS, u=2, e=2))
+
+        def load_w(g):
+            nc.sync.dma_start(
+                out=w_sb[:, g].rearrange(SLABS, u=2),
+                in_=Wv[K_PASS * g : K_PASS * (g + 1), :].rearrange(ROWS, u=2, e=2),
+            )
+
+        load_att(0)
+        load_w(0)
+        load_x(0)
+        load_att(1)
+        load_w(1)
+        load_att(2)
+        nc.sync.dma_start(out=bias[:], in_=bv.partition_broadcast(P))
+        load_att(3)
+        load_x(1)
+        for i in range(4, HEADS):
+            load_att(i)
+
+        c_eye = resident.tile([P, H], F32)
+        c_att = resident.tile([P, H], F32)
+        c_sq = resident.tile([P, H], F32)
+        nc.vector.tensor_copy(out=c_eye[:], in_=w0_bf[:])
+        nc.vector.tensor_tensor(out=c_att[:], in0=w1_bf[:], in1=wk_bf[:], op=SUBTRACT)
+        nc.vector.tensor_scalar(out=c_sq[:], in0=wk_bf[:], scalar1=2.0, scalar2=None, op0=MULT)
+
+        x_codes = resident.tile([P, B, D_PASSES * K_PASS], U32, align_bytes=64)
+        x_scales = resident.tile([P, B, D_PASSES * K_PASS], U8, align_bytes=64)
+        w_codes = resident.tile([P, D_PASSES, D], U32, align_bytes=64)
+        w_scales = resident.tile([P, D_PASSES, D], U8, align_bytes=64)
+        v_codes = resident.tile([P, B, D], U32, align_bytes=64)
+        v_scales = resident.tile([P, B, D], U8, align_bytes=64)
+
+        def quantise(grouped, codes, scales):
+            nc.vector.quantize_mx(out=codes.bitcast(FP8X4), scales=scales, in_=grouped)
+
+        def transpose_words(src, pool, tag):
+            banks = []
+            for j in range(2):
+                bank = pool.tile([P, 2, 2 * P], F32, tag=tag)
+                for u in range(2):
+                    for s in range(2):
+                        words = src[:, 2 * j + s, :].bitcast(F32)
+                        nc.tensor.transpose(
+                            bank[:, u, P * s : P * (s + 1)], words[:, P * u : P * (u + 1)], ident[:]
+                        )
+                banks.append(bank)
+            return banks
+
+        def pack_words(copy, banks, grouped):
+            words = grouped.bitcast(F32)
+            for j in range(2):
+                copy(
+                    out=words[:, K_PASS * j : K_PASS * (j + 1)].rearrange("p (c u) -> p c u", u=2),
+                    in_=banks[j][:].rearrange("p u c -> p c u"),
+                )
+
+        def mx(acc, lhs_codes, lhs_scales, rhs_codes, rhs_scales, start, stop):
+            nc.tensor.matmul_mx(
+                out=acc,
+                lhsT=lhs_codes.bitcast(FP8X4),
+                lhsT_scale=lhs_scales,
+                rhs=rhs_codes.bitcast(FP8X4),
+                rhs_scale=rhs_scales,
+                start=start,
+                stop=stop,
+            )
+
+        def quantise_x(b, copy):
+            x_wide = wide_pool.tile([P, D_PASSES, UNIT], BF16, tag="wide", align_bytes=64)
+            for g in range(D_PASSES):
+                banks = transpose_words(x_sb[b][:, :, K_PASS * g : K_PASS * (g + 1)], mx_pool, "mx")
+                pack_words(copy, banks, x_wide[:, g, :])
+            quantise(x_wide[:].rearrange("p g c -> p (g c)"), x_codes[:, b, :], x_scales[:, b, :])
+
+        def quantise_w(g):
+            w_wide = wide_pool.tile([P, 2 * UNIT], BF16, tag="wide", align_bytes=64)
+            nc.vector.tensor_copy(
+                out=w_wide[:].rearrange("p (c i t) -> p c t i", i=4, t=PACK),
+                in_=w_sb[:, g].rearrange("p t (c i) -> p c t i", i=4),
+            )
+            quantise(w_wide[:], w_codes[:, g, :], w_scales[:, g, :])
+
+        banks_of = [None] * HEADS
+        pair_of = [None] * HEADS
+        scaled_of = [None] * HEADS
+        codes_of = [None] * HEADS
+        gf_of = [None] * HEADS
+        v_of = [None] * HEADS
+
+        def transpose_att(i):
+            banks_of[i] = transpose_words(att_sb[i], tp_pool, "tp")
+
+        def regroup_right(copy, i, tiles):
+            for t in tiles:
+                u, e = t // 2, t % 2
+                copy(
+                    out=pair_of[i][:, 0, K_PASS * t : K_PASS * (t + 1)].rearrange(
+                        "p (q t) -> p q t", t=PACK
+                    ),
+                    in_=att_sb[i][:, :, 2 * P * u : 2 * P * (u + 1)].rearrange(
+                        "p t (q e) -> p e q t", e=2
+                    )[:, e],
+                )
+
+        def unpack(i):
+            h = i % H
+            pair = pair_pool.tile([P, 2, UNIT], BF16, tag="pair", align_bytes=64)
+            pair_of[i] = pair
+            pack_words(nc.scalar.copy, banks_of[i], pair[:, 1, :])
+            at = scaled_pool.tile([P, PACK * DIAG_STEP], F32, tag="scaled")
+            scaled_of[i] = at
+            slabs = at[:, 0 : PACK * N].rearrange("p (t n) -> p t n", t=PACK)
+            for j in range(2):
+                nc.scalar.activation(
+                    out=slabs[:, :, 2 * P * j : 2 * P * (j + 1)].rearrange(SLABS, u=2),
+                    in_=banks_of[i][j][:].bitcast(BF16).rearrange("p u (c e) -> p u e c", e=2),
+                    func=COPY,
+                    scale=c_att[:, h : h + 1],
+                )
+            regroup_right(nc.scalar.copy, i, range(0, SCALAR_TILES))
+            regroup_right(nc.vector.tensor_copy, i, range(SCALAR_TILES, PACK))
+
+        def quantise_pair(i):
+            h = i % H
+            diag = scaled_of[i][:].rearrange("p (t w) -> p t w", w=DIAG_STEP)[:, :, 0:P]
+            nc.vector.scalar_tensor_tensor(
+                out=diag,
+                in0=ident[:].unsqueeze(1).to_broadcast([P, PACK, P]),
+                scalar=c_eye[:, h : h + 1],
+                in1=diag,
+                op0=MULT,
+                op1=ADD,
+            )
+            codes = work_pool.tile([P, 2, K_PASS], U32, tag="codes", align_bytes=64)
+            scales = work_pool.tile([P, 2, K_PASS], U8, tag="scales", align_bytes=64)
+            quantise(
+                pair_of[i][:].rearrange("p a c -> p (a c)"),
+                codes[:].rearrange("p a c -> p (a c)"),
+                scales[:].rearrange("p a c -> p (a c)"),
+            )
+            codes_of[i] = (codes, scales)
+
+        def project(i):
+            b, h = i // H, i % H
+            head = slice(DH * h, DH * (h + 1))
+            v_acc = mx_pool.tile([P, PACK, DH], F32, tag="mx")
+            for t in range(PACK):
+                for g in range(D_PASSES):
+                    tokens = slice(K_PASS * g + P * t, K_PASS * g + P * (t + 1))
+                    mx(
+                        v_acc[:, t, :],
+                        x_codes[:, b, tokens],
+                        x_scales[:, b, tokens],
+                        w_codes[:, g, head],
+                        w_scales[:, g, head],
+                        g == 0,
+                        g == D_PASSES - 1,
+                    )
+            v_grouped = work_pool.tile([P, DH, PACK], BF16, tag="v_grouped", align_bytes=64)
+            nc.vector.tensor_tensor(
+                out=v_grouped[:],
+                in0=v_acc[:].rearrange("p t d -> p d t"),
+                in1=bias[:, head].unsqueeze(2).to_broadcast([P, DH, PACK]),
+                op=ADD,
+            )
+            v_of[i] = v_grouped
+
+        def quantise_v(i):
+            b, h = i // H, i % H
+            head = slice(DH * h, DH * (h + 1))
+            quantise(v_of[i][:].rearrange("p d t -> p (d t)"), v_codes[:, b, head], v_scales[:, b, head])
+
+        def filter_head(i):
+            h = i % H
+            codes, scales = codes_of[i]
+            slabs = scaled_of[i][:, 0 : PACK * N].rearrange("p (t n) -> p t n", t=PACK)
+            gf_grouped = work_pool.tile([P, UNIT], BF16, tag="gf_grouped", align_bytes=64)
+            for c in range(N // P):
+                queries = slice(P * c, P * (c + 1))
+                sq = mx_pool.tile([P, PACK, P], F32, tag="mx")
+                for t in range(PACK):
+                    keys = slice(P * t, P * (t + 1))
+                    mx(
+                        sq[:, t, :],
+                        codes[:, 0, keys],
+                        scales[:, 0, keys],
+                        codes[:, 1, queries],
+                        scales[:, 1, queries],
+                        True,
+                        True,
+                    )
+                nc.vector.scalar_tensor_tensor(
+                    out=gf_grouped[:, K_PASS * c : K_PASS * (c + 1)].rearrange(
+                        "p (n t) -> p n t", t=PACK
+                    ),
+                    in0=sq[:].rearrange("p t n -> p n t"),
+                    scalar=c_sq[:, h : h + 1],
+                    in1=slabs[:, :, queries].rearrange("p t n -> p n t"),
+                    op0=MULT,
+                    op1=ADD,
+                )
+            gf_of[i] = gf_grouped
+
+        def apply_head(i):
+            b, h = i // H, i % H
+            head = slice(DH * h, DH * (h + 1))
+            g_codes = work_pool.tile([P, K_PASS], U32, tag="g_codes", align_bytes=64)
+            g_scales = work_pool.tile([P, K_PASS], U8, tag="g_scales", align_bytes=64)
+            quantise(gf_of[i][:], g_codes[:], g_scales[:])
+            o_acc = mx_pool.tile([P, PACK, DH], F32, tag="mx")
+            for t in range(PACK):
+                queries = slice(P * t, P * (t + 1))
+                mx(
+                    o_acc[:, t, :],
+                    g_codes[:, queries],
+                    g_scales[:, queries],
+                    v_codes[:, b, head],
+                    v_scales[:, b, head],
+                    True,
+                    True,
+                )
+            o_sb = out_pool.tile([P, PACK, DH], F32, tag="o_sb")
+            nc.scalar.copy(out=o_sb[:], in_=o_acc[:])
+            rows = out[b].rearrange(ROWS, u=2, e=2)
+            for u in range(2):
+                nc.sync.dma_start(out=rows[:, u, :, head], in_=o_sb[:, 2 * u : 2 * (u + 1), :])
+
+        def is_head(i):
+            return 0 <= i < HEADS
+
+        transpose_att(0)
+        for step in range(HEADS + 3):
+            if is_head(step + 1):
+                transpose_att(step + 1)
+            if is_head(step):
+                unpack(step)
+            if step == 0:
+                quantise_w(0)
+                quantise_x(0, nc.vector.tensor_copy)
+                quantise_w(1)
+            if step == H // 2:
+                quantise_x(1, nc.scalar.copy)
+            if is_head(step - 3):
+                apply_head(step - 3)
+            if is_head(step - 1):
+                quantise_pair(step - 1)
+            if is_head(step - 2):
+                project(step - 2)
+                filter_head(step - 2)
+                quantise_v(step - 2)

@@ -20,7 +20,7 @@ B, N, D, H, DH = 2, 512, 1024, 8, 128
 HEADS = B * H
 D_PASSES = D // K_PASS
 UNIT = K_PASS * PACK
-SCALAR_TILES = 3
+SCALAR_PAIRS = 64
 DIAG_STEP = N + P
 
 FLOPS = 2 * B * N * D * D + HEADS * 2 * N * N * N + HEADS * 2 * N * N * DH
@@ -39,7 +39,8 @@ def tile_gfsa_pa_kernel(tc, x, att, Wv, bv, w0, w1, wK, out):
         work_pool = ctx.enter_context(tc.tile_pool(name="work", bufs=2))
         out_pool = ctx.enter_context(tc.tile_pool(name="outs", bufs=3))
         tp_pool = ctx.enter_context(tc.psum_pool(name="tp", bufs=4))
-        mx_pool = ctx.enter_context(tc.psum_pool(name="mx", bufs=4))
+        mx_pool = ctx.enter_context(tc.psum_pool(name="mx", bufs=3))
+        o_pool = ctx.enter_context(tc.psum_pool(name="o", bufs=1))
         ctx.enter_context(tc.manual_schedule())
 
         ident = resident.tile([P, P], F32)
@@ -72,16 +73,15 @@ def tile_gfsa_pa_kernel(tc, x, att, Wv, bv, w0, w1, wK, out):
                 in_=Wv[K_PASS * g : K_PASS * (g + 1), :].rearrange(ROWS, u=2, e=2),
             )
 
-        load_att(0)
         load_w(0)
+        load_att(0)
         load_x(0)
-        load_att(1)
         load_w(1)
+        load_att(1)
+        load_x(1)
         load_att(2)
         nc.sync.dma_start(out=bias[:], in_=bv.partition_broadcast(P))
-        load_att(3)
-        load_x(1)
-        for i in range(4, HEADS):
+        for i in range(3, HEADS):
             load_att(i)
 
         c_eye = resident.tile([P, H], F32)
@@ -90,6 +90,13 @@ def tile_gfsa_pa_kernel(tc, x, att, Wv, bv, w0, w1, wK, out):
         nc.vector.tensor_copy(out=c_eye[:], in_=w0_bf[:])
         nc.vector.tensor_tensor(out=c_att[:], in0=w1_bf[:], in1=wk_bf[:], op=SUBTRACT)
         nc.vector.tensor_scalar(out=c_sq[:], in0=wk_bf[:], scalar1=2.0, scalar2=None, op0=MULT)
+        eye = resident.tile([P, H, P], F32)
+        nc.vector.tensor_tensor(
+            out=eye[:],
+            in0=ident[:].unsqueeze(1).to_broadcast([P, H, P]),
+            in1=c_eye[:].unsqueeze(2).to_broadcast([P, H, P]),
+            op=MULT,
+        )
 
         x_codes = resident.tile([P, B, D_PASSES * K_PASS], U32, align_bytes=64)
         x_scales = resident.tile([P, B, D_PASSES * K_PASS], U8, align_bytes=64)
@@ -133,11 +140,11 @@ def tile_gfsa_pa_kernel(tc, x, att, Wv, bv, w0, w1, wK, out):
                 stop=stop,
             )
 
-        def quantise_x(b, copy):
+        def quantise_x(b):
             x_wide = wide_pool.tile([P, D_PASSES, UNIT], BF16, tag="wide", align_bytes=64)
             for g in range(D_PASSES):
                 banks = transpose_words(x_sb[b][:, :, K_PASS * g : K_PASS * (g + 1)], mx_pool, "mx")
-                pack_words(copy, banks, x_wide[:, g, :])
+                pack_words(nc.vector.tensor_copy, banks, x_wide[:, g, :])
             quantise(x_wide[:].rearrange("p g c -> p (g c)"), x_codes[:, b, :], x_scales[:, b, :])
 
         def quantise_w(g):
@@ -154,21 +161,15 @@ def tile_gfsa_pa_kernel(tc, x, att, Wv, bv, w0, w1, wK, out):
         codes_of = [None] * HEADS
         gf_of = [None] * HEADS
         v_of = [None] * HEADS
+        o_of = [None] * HEADS
 
         def transpose_att(i):
             banks_of[i] = transpose_words(att_sb[i], tp_pool, "tp")
 
-        def regroup_right(copy, i, tiles):
-            for t in tiles:
-                u, e = t // 2, t % 2
-                copy(
-                    out=pair_of[i][:, 0, K_PASS * t : K_PASS * (t + 1)].rearrange(
-                        "p (q t) -> p q t", t=PACK
-                    ),
-                    in_=att_sb[i][:, :, 2 * P * u : 2 * P * (u + 1)].rearrange(
-                        "p t (q e) -> p e q t", e=2
-                    )[:, e],
-                )
+        def regroup_right(copy, i, u, pairs):
+            tiles = pair_of[i][:, 0, :].rearrange("p (u e q t) -> p u q e t", u=2, e=2, t=PACK)
+            keys = att_sb[i][:].rearrange("p t (u q e) -> p u q e t", u=2, e=2)
+            copy(out=tiles[:, u, pairs], in_=keys[:, u, pairs])
 
         def unpack(i):
             h = i % H
@@ -185,19 +186,15 @@ def tile_gfsa_pa_kernel(tc, x, att, Wv, bv, w0, w1, wK, out):
                     func=COPY,
                     scale=c_att[:, h : h + 1],
                 )
-            regroup_right(nc.scalar.copy, i, range(0, SCALAR_TILES))
-            regroup_right(nc.vector.tensor_copy, i, range(SCALAR_TILES, PACK))
+            regroup_right(nc.scalar.copy, i, 0, slice(0, P))
+            regroup_right(nc.scalar.copy, i, 1, slice(0, SCALAR_PAIRS))
+            regroup_right(nc.vector.tensor_copy, i, 1, slice(SCALAR_PAIRS, P))
 
         def quantise_pair(i):
             h = i % H
             diag = scaled_of[i][:].rearrange("p (t w) -> p t w", w=DIAG_STEP)[:, :, 0:P]
-            nc.vector.scalar_tensor_tensor(
-                out=diag,
-                in0=ident[:].unsqueeze(1).to_broadcast([P, PACK, P]),
-                scalar=c_eye[:, h : h + 1],
-                in1=diag,
-                op0=MULT,
-                op1=ADD,
+            nc.gpsimd.tensor_tensor(
+                out=diag, in0=diag, in1=eye[:, h, :].unsqueeze(1).to_broadcast([P, PACK, P]), op=ADD
             )
             codes = work_pool.tile([P, 2, K_PASS], U32, tag="codes", align_bytes=64)
             scales = work_pool.tile([P, 2, K_PASS], U8, tag="scales", align_bytes=64)
@@ -275,7 +272,7 @@ def tile_gfsa_pa_kernel(tc, x, att, Wv, bv, w0, w1, wK, out):
             g_codes = work_pool.tile([P, K_PASS], U32, tag="g_codes", align_bytes=64)
             g_scales = work_pool.tile([P, K_PASS], U8, tag="g_scales", align_bytes=64)
             quantise(gf_of[i][:], g_codes[:], g_scales[:])
-            o_acc = mx_pool.tile([P, PACK, DH], F32, tag="mx")
+            o_acc = o_pool.tile([P, PACK, DH], F32, tag="o")
             for t in range(PACK):
                 queries = slice(P * t, P * (t + 1))
                 mx(
@@ -287,8 +284,13 @@ def tile_gfsa_pa_kernel(tc, x, att, Wv, bv, w0, w1, wK, out):
                     True,
                     True,
                 )
+            o_of[i] = o_acc
+
+        def store_head(i):
+            b, h = i // H, i % H
+            head = slice(DH * h, DH * (h + 1))
             o_sb = out_pool.tile([P, PACK, DH], F32, tag="o_sb")
-            nc.scalar.copy(out=o_sb[:], in_=o_acc[:])
+            nc.scalar.copy(out=o_sb[:], in_=o_of[i][:])
             rows = out[b].rearrange(ROWS, u=2, e=2)
             for u in range(2):
                 nc.sync.dma_start(out=rows[:, u, :, head], in_=o_sb[:, 2 * u : 2 * (u + 1), :])
@@ -297,17 +299,19 @@ def tile_gfsa_pa_kernel(tc, x, att, Wv, bv, w0, w1, wK, out):
             return 0 <= i < HEADS
 
         transpose_att(0)
-        for step in range(HEADS + 3):
+        for step in range(HEADS + 5):
+            if step == 0:
+                quantise_w(0)
             if is_head(step + 1):
                 transpose_att(step + 1)
+            if is_head(step - 4):
+                store_head(step - 4)
             if is_head(step):
                 unpack(step)
             if step == 0:
-                quantise_w(0)
-                quantise_x(0, nc.vector.tensor_copy)
+                quantise_x(0)
                 quantise_w(1)
-            if step == H // 2:
-                quantise_x(1, nc.scalar.copy)
+                quantise_x(1)
             if is_head(step - 3):
                 apply_head(step - 3)
             if is_head(step - 1):

@@ -312,11 +312,11 @@ def tile_gfsa_pa_kernel(tc, x, att, Wv, bv, w0, w1, wK, out):
                 quantise_x(0)
                 quantise_w(1)
                 quantise_x(1)
-            if is_head(step - 3):
-                apply_head(step - 3)
             if is_head(step - 1):
                 quantise_pair(step - 1)
             if is_head(step - 2):
                 project(step - 2)
                 filter_head(step - 2)
                 quantise_v(step - 2)
+            if is_head(step - 3):
+                apply_head(step - 3)

@@ -162,6 +162,7 @@ def tile_gfsa_pa_kernel(tc, x, att, Wv, bv, w0, w1, wK, out):
         gf_of = [None] * HEADS
         v_of = [None] * HEADS
         o_of = [None] * HEADS
+        gf_codes_of = [None] * HEADS
 
         def transpose_att(i):
             banks_of[i] = transpose_words(att_sb[i], tp_pool, "tp")
@@ -266,12 +267,16 @@ def tile_gfsa_pa_kernel(tc, x, att, Wv, bv, w0, w1, wK, out):
                 )
             gf_of[i] = gf_grouped
 
+        def quantise_gf(i):
+            g_codes = work_pool.tile([P, K_PASS], U32, tag="g_codes", bufs=3, align_bytes=64)
+            g_scales = work_pool.tile([P, K_PASS], U8, tag="g_scales", bufs=3, align_bytes=64)
+            quantise(gf_of[i][:], g_codes[:], g_scales[:])
+            gf_codes_of[i] = (g_codes, g_scales)
+
         def apply_head(i):
             b, h = i // H, i % H
             head = slice(DH * h, DH * (h + 1))
-            g_codes = work_pool.tile([P, K_PASS], U32, tag="g_codes", align_bytes=64)
-            g_scales = work_pool.tile([P, K_PASS], U8, tag="g_scales", align_bytes=64)
-            quantise(gf_of[i][:], g_codes[:], g_scales[:])
+            g_codes, g_scales = gf_codes_of[i]
             o_acc = o_pool.tile([P, PACK, DH], F32, tag="o")
             for t in range(PACK):
                 queries = slice(P * t, P * (t + 1))
@@ -299,24 +304,25 @@ def tile_gfsa_pa_kernel(tc, x, att, Wv, bv, w0, w1, wK, out):
             return 0 <= i < HEADS
 
         transpose_att(0)
-        for step in range(HEADS + 5):
+        for step in range(HEADS + 6):
             if step == 0:
                 quantise_w(0)
             if is_head(step + 1):
                 transpose_att(step + 1)
-            if is_head(step - 4):
-                store_head(step - 4)
+            if is_head(step - 5):
+                store_head(step - 5)
             if is_head(step):
                 unpack(step)
             if step == 0:
                 quantise_x(0)
                 quantise_w(1)
                 quantise_x(1)
+            if is_head(step - 4):
+                apply_head(step - 4)
             if is_head(step - 1):
                 quantise_pair(step - 1)
             if is_head(step - 2):
                 project(step - 2)
                 filter_head(step - 2)
                 quantise_v(step - 2)
-            if is_head(step - 3):
-                apply_head(step - 3)
+                quantise_gf(step - 2)

@@ -172,6 +172,9 @@ def tile_gfsa_pa_kernel(tc, x, att, Wv, bv, w0, w1, wK, out):
             keys = att_sb[i][:].rearrange("p t (u q e) -> p u q e t", u=2, e=2)
             copy(out=tiles[:, u, pairs], in_=keys[:, u, pairs])
 
+        def gpsimd_copy(out, in_):
+            nc.gpsimd.tensor_scalar(out=out, in0=in_, scalar1=1.0, scalar2=0.0, op0=MULT, op1=ADD)
+
         def unpack(i):
             h = i % H
             pair = pair_pool.tile([P, 2, UNIT], BF16, tag="pair", align_bytes=64)
@@ -189,7 +192,7 @@ def tile_gfsa_pa_kernel(tc, x, att, Wv, bv, w0, w1, wK, out):
                 )
             regroup_right(nc.scalar.copy, i, 0, slice(0, P))
             regroup_right(nc.scalar.copy, i, 1, slice(0, SCALAR_PAIRS))
-            regroup_right(nc.vector.tensor_copy, i, 1, slice(SCALAR_PAIRS, P))
+            regroup_right(gpsimd_copy, i, 1, slice(SCALAR_PAIRS, P))
 
         def quantise_pair(i):
             h = i % H

@@ -20,7 +20,6 @@ B, N, D, H, DH = 2, 512, 1024, 8, 128
 HEADS = B * H
 D_PASSES = D // K_PASS
 UNIT = K_PASS * PACK
-SCALAR_PAIRS = 64
 DIAG_STEP = N + P
 
 FLOPS = 2 * B * N * D * D + HEADS * 2 * N * N * N + HEADS * 2 * N * N * DH
@@ -167,10 +166,10 @@ def tile_gfsa_pa_kernel(tc, x, att, Wv, bv, w0, w1, wK, out):
         def transpose_att(i):
             banks_of[i] = transpose_words(att_sb[i], tp_pool, "tp")
 
-        def regroup_right(copy, i, u, pairs):
+        def regroup_right(copy, i, u):
             tiles = pair_of[i][:, 0, :].rearrange("p (u e q t) -> p u q e t", u=2, e=2, t=PACK)
             keys = att_sb[i][:].rearrange("p t (u q e) -> p u q e t", u=2, e=2)
-            copy(out=tiles[:, u, pairs], in_=keys[:, u, pairs])
+            copy(out=tiles[:, u], in_=keys[:, u])
 
         def gpsimd_copy(out, in_):
             nc.gpsimd.tensor_scalar(out=out, in0=in_, scalar1=1.0, scalar2=0.0, op0=MULT, op1=ADD)
@@ -190,9 +189,8 @@ def tile_gfsa_pa_kernel(tc, x, att, Wv, bv, w0, w1, wK, out):
                     func=COPY,
                     scale=c_att[:, h : h + 1],
                 )
-            regroup_right(nc.scalar.copy, i, 0, slice(0, P))
-            regroup_right(nc.scalar.copy, i, 1, slice(0, SCALAR_PAIRS))
-            regroup_right(gpsimd_copy, i, 1, slice(SCALAR_PAIRS, P))
+            regroup_right(nc.scalar.copy, i, 0)
+            regroup_right(gpsimd_copy, i, 1)
 
         def quantise_pair(i):
             h = i % H
@@ -307,9 +305,9 @@ def tile_gfsa_pa_kernel(tc, x, att, Wv, bv, w0, w1, wK, out):
             return 0 <= i < HEADS
 
         transpose_att(0)
+        quantise_w(0)
+        quantise_x(0)
         for step in range(HEADS + 6):
-            if step == 0:
-                quantise_w(0)
             if is_head(step + 1):
                 transpose_att(step + 1)
             if is_head(step - 5):
@@ -317,7 +315,6 @@ def tile_gfsa_pa_kernel(tc, x, att, Wv, bv, w0, w1, wK, out):
             if is_head(step):
                 unpack(step)
             if step == 0:
-                quantise_x(0)
                 quantise_w(1)
                 quantise_x(1)
             if is_head(step - 4):

@@ -20,6 +20,7 @@ B, N, D, H, DH = 2, 512, 1024, 8, 128
 HEADS = B * H
 D_PASSES = D // K_PASS
 UNIT = K_PASS * PACK
+SCALAR_PAIRS = 64
 DIAG_STEP = N + P
 
 FLOPS = 2 * B * N * D * D + HEADS * 2 * N * N * N + HEADS * 2 * N * N * DH
@@ -166,10 +167,10 @@ def tile_gfsa_pa_kernel(tc, x, att, Wv, bv, w0, w1, wK, out):
         def transpose_att(i):
             banks_of[i] = transpose_words(att_sb[i], tp_pool, "tp")
 
-        def regroup_right(copy, i, u):
+        def regroup_right(copy, i, u, pairs):
             tiles = pair_of[i][:, 0, :].rearrange("p (u e q t) -> p u q e t", u=2, e=2, t=PACK)
             keys = att_sb[i][:].rearrange("p t (u q e) -> p u q e t", u=2, e=2)
-            copy(out=tiles[:, u], in_=keys[:, u])
+            copy(out=tiles[:, u, pairs], in_=keys[:, u, pairs])
 
         def gpsimd_copy(out, in_):
             nc.gpsimd.tensor_scalar(out=out, in0=in_, scalar1=1.0, scalar2=0.0, op0=MULT, op1=ADD)
@@ -189,8 +190,9 @@ def tile_gfsa_pa_kernel(tc, x, att, Wv, bv, w0, w1, wK, out):
                     func=COPY,
                     scale=c_att[:, h : h + 1],
                 )
-            regroup_right(nc.scalar.copy, i, 0)
-            regroup_right(gpsimd_copy, i, 1)
+            regroup_right(nc.scalar.copy, i, 0, slice(0, P))
+            regroup_right(nc.scalar.copy, i, 1, slice(0, SCALAR_PAIRS))
+            regroup_right(gpsimd_copy, i, 1, slice(SCALAR_PAIRS, P))
 
         def quantise_pair(i):
             h = i % H

@@ -49,9 +49,9 @@ def tile_gfsa_pa_kernel(tc, x, att, Wv, bv, w0, w1, wK, out):
         w0_bf = resident.tile([P, H], BF16)
         w1_bf = resident.tile([P, H], BF16)
         wk_bf = resident.tile([P, H], BF16)
-        nc.scalar.dma_start(out=w0_bf[:], in_=w0.partition_broadcast(P))
-        nc.scalar.dma_start(out=w1_bf[:], in_=w1.partition_broadcast(P))
-        nc.scalar.dma_start(out=wk_bf[:], in_=wK.partition_broadcast(P))
+        nc.sync.dma_start(out=w1_bf[:], in_=w1.partition_broadcast(P))
+        nc.sync.dma_start(out=wk_bf[:], in_=wK.partition_broadcast(P))
+        nc.sync.dma_start(out=w0_bf[:], in_=w0.partition_broadcast(P))
 
         x_sb = [resident.tile([P, PACK, D], BF16, name="x_sb%d" % b) for b in range(B)]
         w_sb = resident.tile([P, D_PASSES, PACK, D], BF16)
@@ -73,25 +73,26 @@ def tile_gfsa_pa_kernel(tc, x, att, Wv, bv, w0, w1, wK, out):
                 in_=Wv[K_PASS * g : K_PASS * (g + 1), :].rearrange(ROWS, u=2, e=2),
             )
 
-        load_w(0)
         load_att(0)
+        load_w(0)
         load_x(0)
         load_w(1)
         load_att(1)
-        load_x(1)
-        load_att(2)
         nc.sync.dma_start(out=bias[:], in_=bv.partition_broadcast(P))
-        for i in range(3, HEADS):
+        load_att(2)
+        load_att(3)
+        load_x(1)
+        for i in range(4, HEADS):
             load_att(i)
 
         c_eye = resident.tile([P, H], F32)
         c_att = resident.tile([P, H], F32)
         c_sq = resident.tile([P, H], F32)
-        nc.vector.tensor_copy(out=c_eye[:], in_=w0_bf[:])
         nc.vector.tensor_tensor(out=c_att[:], in0=w1_bf[:], in1=wk_bf[:], op=SUBTRACT)
         nc.vector.tensor_scalar(out=c_sq[:], in0=wk_bf[:], scalar1=2.0, scalar2=None, op0=MULT)
+        nc.gpsimd.tensor_copy(out=c_eye[:], in_=w0_bf[:])
         eye = resident.tile([P, H, P], F32)
-        nc.vector.tensor_tensor(
+        nc.gpsimd.tensor_tensor(
             out=eye[:],
             in0=ident[:].unsqueeze(1).to_broadcast([P, H, P]),
             in1=c_eye[:].unsqueeze(2).to_broadcast([P, H, P]),
@@ -140,12 +141,16 @@ def tile_gfsa_pa_kernel(tc, x, att, Wv, bv, w0, w1, wK, out):
                 stop=stop,
             )
 
+        def regroup_x(b, g, copy):
+            if g == 0:
+                x_wide_of[b] = wide_pool.tile(
+                    [P, D_PASSES, UNIT], BF16, name="x_wide", tag="wide", align_bytes=64
+                )
+            banks = transpose_words(x_sb[b][:, :, K_PASS * g : K_PASS * (g + 1)], mx_pool, "mx")
+            pack_words(copy, banks, x_wide_of[b][:, g, :])
+
         def quantise_x(b):
-            x_wide = wide_pool.tile([P, D_PASSES, UNIT], BF16, tag="wide", align_bytes=64)
-            for g in range(D_PASSES):
-                banks = transpose_words(x_sb[b][:, :, K_PASS * g : K_PASS * (g + 1)], mx_pool, "mx")
-                pack_words(nc.vector.tensor_copy, banks, x_wide[:, g, :])
-            quantise(x_wide[:].rearrange("p g c -> p (g c)"), x_codes[:, b, :], x_scales[:, b, :])
+            quantise(x_wide_of[b][:].rearrange("p g c -> p (g c)"), x_codes[:, b, :], x_scales[:, b, :])
 
         def quantise_w(g):
             w_wide = wide_pool.tile([P, 2 * UNIT], BF16, tag="wide", align_bytes=64)
@@ -155,6 +160,7 @@ def tile_gfsa_pa_kernel(tc, x, att, Wv, bv, w0, w1, wK, out):
             )
             quantise(w_wide[:], w_codes[:, g, :], w_scales[:, g, :])
 
+        x_wide_of = [None] * B
         banks_of = [None] * HEADS
         pair_of = [None] * HEADS
         scaled_of = [None] * HEADS
@@ -179,7 +185,7 @@ def tile_gfsa_pa_kernel(tc, x, att, Wv, bv, w0, w1, wK, out):
             h = i % H
             pair = pair_pool.tile([P, 2, UNIT], BF16, tag="pair", align_bytes=64)
             pair_of[i] = pair
-            pack_words(nc.scalar.copy, banks_of[i], pair[:, 1, :])
+            pack_words(nc.vector.tensor_copy if i == 0 else nc.scalar.copy, banks_of[i], pair[:, 1, :])
             at = scaled_pool.tile([P, PACK * DIAG_STEP], F32, tag="scaled")
             scaled_of[i] = at
             slabs = at[:, 0 : PACK * N].rearrange("p (t n) -> p t n", t=PACK)
@@ -307,17 +313,23 @@ def tile_gfsa_pa_kernel(tc, x, att, Wv, bv, w0, w1, wK, out):
             return 0 <= i < HEADS
 
         transpose_att(0)
-        quantise_w(0)
-        quantise_x(0)
         for step in range(HEADS + 6):
-            if is_head(step + 1):
+            if step > 0 and is_head(step + 1):
                 transpose_att(step + 1)
             if is_head(step - 5):
                 store_head(step - 5)
             if is_head(step):
                 unpack(step)
             if step == 0:
+                quantise_w(0)
+                regroup_x(0, 0, nc.vector.tensor_copy)
+                regroup_x(0, 1, nc.vector.tensor_copy)
+                quantise_x(0)
+                transpose_att(1)
                 quantise_w(1)
+            if 5 <= step < 5 + D_PASSES:
+                regroup_x(1, step - 5, nc.vector.tensor_copy)
+            if step == 7:
                 quantise_x(1)
             if is_head(step - 4):
                 apply_head(step - 4)

@@ -38,13 +38,16 @@ def tile_gfsa_pa_kernel(tc, x, att, Wv, bv, w0, w1, wK, out):
         scaled_pool = ctx.enter_context(tc.tile_pool(name="scaled", bufs=3))
         work_pool = ctx.enter_context(tc.tile_pool(name="work", bufs=2))
         out_pool = ctx.enter_context(tc.tile_pool(name="outs", bufs=3))
-        tp_pool = ctx.enter_context(tc.psum_pool(name="tp", bufs=4))
+        tp_pool = ctx.enter_context(tc.psum_pool(name="tp", bufs=3))
+        right_pool = ctx.enter_context(tc.psum_pool(name="right", bufs=1))
         mx_pool = ctx.enter_context(tc.psum_pool(name="mx", bufs=3))
         o_pool = ctx.enter_context(tc.psum_pool(name="o", bufs=1))
         ctx.enter_context(tc.manual_schedule())
 
         ident = resident.tile([P, P], F32)
         make_identity(nc, ident[:])
+        ident_bf = resident.tile([P, P], BF16)
+        nc.gpsimd.tensor_copy(out=ident_bf[:], in_=ident[:])
 
         w0_bf = resident.tile([P, H], BF16)
         w1_bf = resident.tile([P, H], BF16)
@@ -162,6 +165,7 @@ def tile_gfsa_pa_kernel(tc, x, att, Wv, bv, w0, w1, wK, out):
 
         x_wide_of = [None] * B
         banks_of = [None] * HEADS
+        right_of = [None] * HEADS
         pair_of = [None] * HEADS
         scaled_of = [None] * HEADS
         codes_of = [None] * HEADS
@@ -171,6 +175,16 @@ def tile_gfsa_pa_kernel(tc, x, att, Wv, bv, w0, w1, wK, out):
         gf_codes_of = [None] * HEADS
 
         def transpose_att(i):
+            bank = right_pool.tile([P, 2, P, PACK], BF16, tag="right")
+            for t in range(0, PACK, 2):
+                nc.tensor.matmul(
+                    bank[:, :, :, t : t + 2],
+                    lhsT=ident_bf[:],
+                    rhs=att_sb[i][:, t : t + 2, 0 : 2 * P].rearrange("p t (q e) -> p e q t", e=2),
+                    start=True,
+                    stop=True,
+                )
+            right_of[i] = bank
             banks_of[i] = transpose_words(att_sb[i], tp_pool, "tp")
 
         def regroup_right(copy, i, u, pairs):
@@ -185,6 +199,9 @@ def tile_gfsa_pa_kernel(tc, x, att, Wv, bv, w0, w1, wK, out):
             h = i % H
             pair = pair_pool.tile([P, 2, UNIT], BF16, tag="pair", align_bytes=64)
             pair_of[i] = pair
+            nc.scalar.copy(
+                out=pair[:, 0, 0 : UNIT // 2], in_=right_of[i][:].rearrange("p e q t -> p (e q t)")
+            )
             pack_words(nc.vector.tensor_copy if i == 0 else nc.scalar.copy, banks_of[i], pair[:, 1, :])
             at = scaled_pool.tile([P, PACK * DIAG_STEP], F32, tag="scaled")
             scaled_of[i] = at
@@ -196,7 +213,6 @@ def tile_gfsa_pa_kernel(tc, x, att, Wv, bv, w0, w1, wK, out):
                     func=COPY,
                     scale=c_att[:, h : h + 1],
                 )
-            regroup_right(nc.scalar.copy, i, 0, slice(0, P))
             regroup_right(nc.scalar.copy, i, 1, slice(0, SCALAR_PAIRS))
             regroup_right(gpsimd_copy, i, 1, slice(SCALAR_PAIRS, P))
 
@@ -245,12 +261,14 @@ def tile_gfsa_pa_kernel(tc, x, att, Wv, bv, w0, w1, wK, out):
             head = slice(DH * h, DH * (h + 1))
             quantise(v_of[i][:].rearrange("p d t -> p (d t)"), v_codes[:, b, head], v_scales[:, b, head])
 
-        def filter_head(i):
+        def filter_head(i, halfway):
             h = i % H
             codes, scales = codes_of[i]
             slabs = scaled_of[i][:, 0 : PACK * N].rearrange("p (t n) -> p t n", t=PACK)
             gf_grouped = work_pool.tile([P, UNIT], BF16, tag="gf_grouped", align_bytes=64)
             for c in range(N // P):
+                if c == 2:
+                    halfway()
                 queries = slice(P * c, P * (c + 1))
                 sq = mx_pool.tile([P, PACK, P], F32, tag="mx")
                 for t in range(PACK):
@@ -314,8 +332,6 @@ def tile_gfsa_pa_kernel(tc, x, att, Wv, bv, w0, w1, wK, out):
 
         transpose_att(0)
         for step in range(HEADS + 6):
-            if step > 0 and is_head(step + 1):
-                transpose_att(step + 1)
             if is_head(step - 5):
                 store_head(step - 5)
             if is_head(step):
@@ -331,12 +347,14 @@ def tile_gfsa_pa_kernel(tc, x, att, Wv, bv, w0, w1, wK, out):
                 regroup_x(1, step - 5, nc.vector.tensor_copy)
             if step == 7:
                 quantise_x(1)
+            if step == 1:
+                transpose_att(2)
             if is_head(step - 4):
                 apply_head(step - 4)
             if is_head(step - 1):
                 quantise_pair(step - 1)
             if is_head(step - 2):
                 project(step - 2)
-                filter_head(step - 2)
+                filter_head(step - 2, lambda: transpose_att(step + 1) if is_head(step + 1) else None)
                 quantise_v(step - 2)
                 quantise_gf(step - 2)

@@ -21,12 +21,15 @@ HEADS = B * H
 D_PASSES = D // K_PASS
 UNIT = K_PASS * PACK
 SCALAR_PAIRS = 64
-DIAG_STEP = N + P
 
 FLOPS = 2 * B * N * D * D + HEADS * 2 * N * N * N + HEADS * 2 * N * N * DH
 
+DIAG_STEP = N + P
+
 ROWS = "(u q e) c -> q u e c"
 SLABS = "p (u e) c -> p u e c"
+FROM = "p t (c i) -> p c t i"
+INTO = "p (c i t) -> p c t i"
 
 
 def tile_gfsa_pa_kernel(tc, x, att, Wv, bv, w0, w1, wK, out):
@@ -35,7 +38,7 @@ def tile_gfsa_pa_kernel(tc, x, att, Wv, bv, w0, w1, wK, out):
         resident = ctx.enter_context(tc.tile_pool(name="resident", bufs=1))
         wide_pool = ctx.enter_context(tc.tile_pool(name="wide", bufs=2))
         pair_pool = ctx.enter_context(tc.tile_pool(name="pair", bufs=3))
-        scaled_pool = ctx.enter_context(tc.tile_pool(name="scaled", bufs=3))
+        scaled_pool = ctx.enter_context(tc.tile_pool(name="scaled", bufs=4))
         work_pool = ctx.enter_context(tc.tile_pool(name="work", bufs=2))
         out_pool = ctx.enter_context(tc.tile_pool(name="outs", bufs=3))
         tp_pool = ctx.enter_context(tc.psum_pool(name="tp", bufs=3))
@@ -79,10 +82,10 @@ def tile_gfsa_pa_kernel(tc, x, att, Wv, bv, w0, w1, wK, out):
         load_att(0)
         load_w(0)
         load_x(0)
-        load_w(1)
         load_att(1)
-        nc.sync.dma_start(out=bias[:], in_=bv.partition_broadcast(P))
+        load_w(1)
         load_att(2)
+        nc.sync.dma_start(out=bias[:], in_=bv.partition_broadcast(P))
         load_att(3)
         load_x(1)
         for i in range(4, HEADS):
@@ -112,26 +115,21 @@ def tile_gfsa_pa_kernel(tc, x, att, Wv, bv, w0, w1, wK, out):
         def quantise(grouped, codes, scales):
             nc.vector.quantize_mx(out=codes.bitcast(FP8X4), scales=scales, in_=grouped)
 
-        def transpose_words(src, pool, tag):
-            banks = []
-            for j in range(2):
-                bank = pool.tile([P, 2, 2 * P], F32, tag=tag)
-                for u in range(2):
-                    for s in range(2):
-                        words = src[:, 2 * j + s, :].bitcast(F32)
-                        nc.tensor.transpose(
-                            bank[:, u, P * s : P * (s + 1)], words[:, P * u : P * (u + 1)], ident[:]
-                        )
-                banks.append(bank)
-            return banks
+        def transpose_bank(src, j, pool, tag):
+            bank = pool.tile([P, 2, 2 * P], F32, name="bank", tag=tag)
+            for u in range(2):
+                for s in range(2):
+                    words = src[:, 2 * j + s, :].bitcast(F32)
+                    nc.tensor.transpose(
+                        bank[:, u, P * s : P * (s + 1)], words[:, P * u : P * (u + 1)], ident[:]
+                    )
+            return bank
 
-        def pack_words(copy, banks, grouped):
-            words = grouped.bitcast(F32)
-            for j in range(2):
-                copy(
-                    out=words[:, K_PASS * j : K_PASS * (j + 1)].rearrange("p (c u) -> p c u", u=2),
-                    in_=banks[j][:].rearrange("p u c -> p c u"),
-                )
+        def pack_bank(copy, bank, j, grouped):
+            copy(
+                out=grouped.bitcast(F32)[:, K_PASS * j : K_PASS * (j + 1)].rearrange("p (c u) -> p c u", u=2),
+                in_=bank[:].rearrange("p u c -> p c u"),
+            )
 
         def mx(acc, lhs_codes, lhs_scales, rhs_codes, rhs_scales, start, stop):
             nc.tensor.matmul_mx(
@@ -144,26 +142,32 @@ def tile_gfsa_pa_kernel(tc, x, att, Wv, bv, w0, w1, wK, out):
                 stop=stop,
             )
 
-        def regroup_x(b, g, copy):
-            if g == 0:
+        def transpose_x(b, k, pool, tag):
+            g, j = divmod(k, 2)
+            return transpose_bank(x_sb[b][:, :, K_PASS * g : K_PASS * (g + 1)], j, pool, tag)
+
+        def unpack_x(b, k, bank):
+            g, j = divmod(k, 2)
+            if k == 0:
                 x_wide_of[b] = wide_pool.tile(
                     [P, D_PASSES, UNIT], BF16, name="x_wide", tag="wide", align_bytes=64
                 )
-            banks = transpose_words(x_sb[b][:, :, K_PASS * g : K_PASS * (g + 1)], mx_pool, "mx")
-            pack_words(copy, banks, x_wide_of[b][:, g, :])
+            pack_bank(nc.scalar.copy, bank, j, x_wide_of[b][:, g, :])
 
         def quantise_x(b):
             quantise(x_wide_of[b][:].rearrange("p g c -> p (g c)"), x_codes[:, b, :], x_scales[:, b, :])
 
-        def quantise_w(g):
-            w_wide = wide_pool.tile([P, 2 * UNIT], BF16, tag="wide", align_bytes=64)
+        def regroup_w(g):
+            w_wide_of[g] = wide_pool.tile([P, 2 * UNIT], BF16, name="w_wide", tag="wide", align_bytes=64)
             nc.vector.tensor_copy(
-                out=w_wide[:].rearrange("p (c i t) -> p c t i", i=4, t=PACK),
-                in_=w_sb[:, g].rearrange("p t (c i) -> p c t i", i=4),
+                out=w_wide_of[g][:].rearrange(INTO, i=4, t=PACK), in_=w_sb[:, g].rearrange(FROM, i=4)
             )
-            quantise(w_wide[:], w_codes[:, g, :], w_scales[:, g, :])
+
+        def quantise_w(g):
+            quantise(w_wide_of[g][:], w_codes[:, g, :], w_scales[:, g, :])
 
         x_wide_of = [None] * B
+        w_wide_of = [None] * D_PASSES
         banks_of = [None] * HEADS
         right_of = [None] * HEADS
         pair_of = [None] * HEADS
@@ -175,6 +179,7 @@ def tile_gfsa_pa_kernel(tc, x, att, Wv, bv, w0, w1, wK, out):
         gf_codes_of = [None] * HEADS
 
         def transpose_att(i):
+            banks_of[i] = [transpose_bank(att_sb[i], j, tp_pool, "tp") for j in range(2)]
             bank = right_pool.tile([P, 2, P, PACK], BF16, tag="right")
             for t in range(0, PACK, 2):
                 nc.tensor.matmul(
@@ -185,7 +190,6 @@ def tile_gfsa_pa_kernel(tc, x, att, Wv, bv, w0, w1, wK, out):
                     stop=True,
                 )
             right_of[i] = bank
-            banks_of[i] = transpose_words(att_sb[i], tp_pool, "tp")
 
         def regroup_right(copy, i, u, pairs):
             tiles = pair_of[i][:, 0, :].rearrange("p (u e q t) -> p u q e t", u=2, e=2, t=PACK)
@@ -195,18 +199,23 @@ def tile_gfsa_pa_kernel(tc, x, att, Wv, bv, w0, w1, wK, out):
         def gpsimd_copy(out, in_):
             nc.gpsimd.tensor_scalar(out=out, in0=in_, scalar1=1.0, scalar2=0.0, op0=MULT, op1=ADD)
 
+        def start_pair(i):
+            pair_of[i] = pair_pool.tile([P, 2, UNIT], BF16, name="pair", tag="pair", align_bytes=64)
+            regroup_right(gpsimd_copy, i, 1, slice(SCALAR_PAIRS, P))
+
         def unpack(i):
             h = i % H
-            pair = pair_pool.tile([P, 2, UNIT], BF16, tag="pair", align_bytes=64)
-            pair_of[i] = pair
-            nc.scalar.copy(
-                out=pair[:, 0, 0 : UNIT // 2], in_=right_of[i][:].rearrange("p e q t -> p (e q t)")
-            )
-            pack_words(nc.vector.tensor_copy if i == 0 else nc.scalar.copy, banks_of[i], pair[:, 1, :])
-            at = scaled_pool.tile([P, PACK * DIAG_STEP], F32, tag="scaled")
+            pair = pair_of[i]
+            at = scaled_pool.tile([P, PACK * N], F32, tag="scaled")
             scaled_of[i] = at
-            slabs = at[:, 0 : PACK * N].rearrange("p (t n) -> p t n", t=PACK)
+            slabs = at[:].rearrange("p (t n) -> p t n", t=PACK)
             for j in range(2):
+                if j == 1:
+                    nc.scalar.copy(
+                        out=pair[:, 0, 0 : UNIT // 2],
+                        in_=right_of[i][:].rearrange("p e q t -> p (e q t)"),
+                    )
+                pack_bank(nc.scalar.copy, banks_of[i][j], j, pair[:, 1, :])
                 nc.scalar.activation(
                     out=slabs[:, :, 2 * P * j : 2 * P * (j + 1)].rearrange(SLABS, u=2),
                     in_=banks_of[i][j][:].bitcast(BF16).rearrange("p u (c e) -> p u e c", e=2),
@@ -214,14 +223,17 @@ def tile_gfsa_pa_kernel(tc, x, att, Wv, bv, w0, w1, wK, out):
                     scale=c_att[:, h : h + 1],
                 )
             regroup_right(nc.scalar.copy, i, 1, slice(0, SCALAR_PAIRS))
-            regroup_right(gpsimd_copy, i, 1, slice(SCALAR_PAIRS, P))
+
+        def add_identity(i):
+            h = i % H
+            diag = scaled_of[i][:, 0 : 3 * DIAG_STEP].rearrange("p (t w) -> p t w", w=DIAG_STEP)[:, :, 0:P]
+            nc.gpsimd.tensor_tensor(
+                out=diag, in0=diag, in1=eye[:, h, :].unsqueeze(1).to_broadcast([P, 3, P]), op=ADD
+            )
+            last = scaled_of[i][:, 3 * DIAG_STEP : PACK * N]
+            nc.gpsimd.tensor_tensor(out=last, in0=last, in1=eye[:, h, :], op=ADD)
 
         def quantise_pair(i):
-            h = i % H
-            diag = scaled_of[i][:].rearrange("p (t w) -> p t w", w=DIAG_STEP)[:, :, 0:P]
-            nc.gpsimd.tensor_tensor(
-                out=diag, in0=diag, in1=eye[:, h, :].unsqueeze(1).to_broadcast([P, PACK, P]), op=ADD
-            )
             codes = work_pool.tile([P, 2, K_PASS], U32, tag="codes", align_bytes=64)
             scales = work_pool.tile([P, 2, K_PASS], U8, tag="scales", align_bytes=64)
             quantise(
@@ -264,7 +276,7 @@ def tile_gfsa_pa_kernel(tc, x, att, Wv, bv, w0, w1, wK, out):
         def filter_head(i, halfway):
             h = i % H
             codes, scales = codes_of[i]
-            slabs = scaled_of[i][:, 0 : PACK * N].rearrange("p (t n) -> p t n", t=PACK)
+            slabs = scaled_of[i][:].rearrange("p (t n) -> p t n", t=PACK)
             gf_grouped = work_pool.tile([P, UNIT], BF16, tag="gf_grouped", align_bytes=64)
             for c in range(N // P):
                 if c == 2:
@@ -330,31 +342,43 @@ def tile_gfsa_pa_kernel(tc, x, att, Wv, bv, w0, w1, wK, out):
         def is_head(i):
             return 0 <= i < HEADS
 
+        for i in range(3):
+            start_pair(i)
         transpose_att(0)
-        for step in range(HEADS + 6):
+        unpack(0)
+        for k in range(2 * D_PASSES):
+            unpack_x(0, k, transpose_x(0, k, mx_pool, "mx"))
+        transpose_att(1)
+        regroup_w(0)
+        quantise_w(0)
+        quantise_pair(0)
+        start_pair(3)
+        add_identity(0)
+        unpack(1)
+        transpose_att(2)
+        regroup_w(1)
+        quantise_w(1)
+        quantise_x(0)
+        x_bank = None
+        for step in range(2, HEADS + 6):
             if is_head(step - 5):
                 store_head(step - 5)
             if is_head(step):
                 unpack(step)
-            if step == 0:
-                quantise_w(0)
-                regroup_x(0, 0, nc.vector.tensor_copy)
-                regroup_x(0, 1, nc.vector.tensor_copy)
-                quantise_x(0)
-                transpose_att(1)
-                quantise_w(1)
-            if 5 <= step < 5 + D_PASSES:
-                regroup_x(1, step - 5, nc.vector.tensor_copy)
-            if step == 7:
+            if x_bank is not None:
+                unpack_x(1, step - 5, x_bank)
+            if step == 9:
                 quantise_x(1)
-            if step == 1:
-                transpose_att(2)
             if is_head(step - 4):
                 apply_head(step - 4)
             if is_head(step - 1):
                 quantise_pair(step - 1)
+                if is_head(step + 2):
+                    start_pair(step + 2)
+                add_identity(step - 1)
             if is_head(step - 2):
                 project(step - 2)
                 filter_head(step - 2, lambda: transpose_att(step + 1) if is_head(step + 1) else None)
+                x_bank = transpose_x(1, step - 4, tp_pool, "tp") if 4 <= step < 8 else None
                 quantise_v(step - 2)
                 quantise_gf(step - 2)

@@ -20,11 +20,13 @@ B, N, D, H, DH = 2, 512, 1024, 8, 128
 HEADS = B * H
 D_PASSES = D // K_PASS
 UNIT = K_PASS * PACK
+EARLY = 1
 SCALAR_PAIRS = 64
 
 FLOPS = 2 * B * N * D * D + HEADS * 2 * N * N * N + HEADS * 2 * N * N * DH
 
-DIAG_STEP = N + P
+SLAB_STEP = N + 4
+DIAG_STEP = SLAB_STEP + P
 
 ROWS = "(u q e) c -> q u e c"
 SLABS = "p (u e) c -> p u e c"
@@ -88,8 +90,18 @@ def tile_gfsa_pa_kernel(tc, x, att, Wv, bv, w0, w1, wK, out):
         nc.sync.dma_start(out=bias[:], in_=bv.partition_broadcast(P))
         load_att(3)
         load_x(1)
-        for i in range(4, HEADS):
-            load_att(i)
+        load_att(4)
+        load_att(5)
+        load_att(6)
+        load_att(7)
+        load_att(8)
+        load_att(9)
+        load_att(10)
+        load_att(11)
+        load_att(12)
+        load_att(13)
+        load_att(14)
+        load_att(15)
 
         c_eye = resident.tile([P, H], F32)
         c_att = resident.tile([P, H], F32)
@@ -97,13 +109,11 @@ def tile_gfsa_pa_kernel(tc, x, att, Wv, bv, w0, w1, wK, out):
         nc.vector.tensor_tensor(out=c_att[:], in0=w1_bf[:], in1=wk_bf[:], op=SUBTRACT)
         nc.vector.tensor_scalar(out=c_sq[:], in0=wk_bf[:], scalar1=2.0, scalar2=None, op0=MULT)
         nc.gpsimd.tensor_copy(out=c_eye[:], in_=w0_bf[:])
-        eye = resident.tile([P, H, P], F32)
-        nc.gpsimd.tensor_tensor(
-            out=eye[:],
-            in0=ident[:].unsqueeze(1).to_broadcast([P, H, P]),
-            in1=c_eye[:].unsqueeze(2).to_broadcast([P, H, P]),
-            op=MULT,
-        )
+        eye = resident.tile([P, H, P], BF16)
+        for h in range(H):
+            nc.gpsimd.tensor_scalar(
+                out=eye[:, h, :], in0=ident[:], scalar1=c_eye[:, h : h + 1], scalar2=0.0, op0=MULT, op1=ADD
+            )
 
         x_codes = resident.tile([P, B, D_PASSES * K_PASS], U32, align_bytes=64)
         x_scales = resident.tile([P, B, D_PASSES * K_PASS], U8, align_bytes=64)
@@ -180,6 +190,8 @@ def tile_gfsa_pa_kernel(tc, x, att, Wv, bv, w0, w1, wK, out):
 
         def transpose_att(i):
             banks_of[i] = [transpose_bank(att_sb[i], j, tp_pool, "tp") for j in range(2)]
+            if i < EARLY:
+                return
             bank = right_pool.tile([P, 2, P, PACK], BF16, tag="right")
             for t in range(0, PACK, 2):
                 nc.tensor.matmul(
@@ -201,16 +213,22 @@ def tile_gfsa_pa_kernel(tc, x, att, Wv, bv, w0, w1, wK, out):
 
         def start_pair(i):
             pair_of[i] = pair_pool.tile([P, 2, UNIT], BF16, name="pair", tag="pair", align_bytes=64)
-            regroup_right(gpsimd_copy, i, 1, slice(SCALAR_PAIRS, P))
+            if i >= EARLY:
+                regroup_right(gpsimd_copy, i, 1, slice(SCALAR_PAIRS, P))
+            else:
+                for u in range(2):
+                    regroup_right(nc.vector.tensor_copy, i, u, slice(0, P))
+
+        def slabs_of(i):
+            return scaled_of[i][:].rearrange("p (t n) -> p t n", t=PACK)[:, :, 0:N]
 
         def unpack(i):
             h = i % H
             pair = pair_of[i]
-            at = scaled_pool.tile([P, PACK * N], F32, tag="scaled")
-            scaled_of[i] = at
-            slabs = at[:].rearrange("p (t n) -> p t n", t=PACK)
+            scaled_of[i] = scaled_pool.tile([P, PACK * SLAB_STEP], F32, name="scaled", tag="scaled")
+            slabs = slabs_of(i)
             for j in range(2):
-                if j == 1:
+                if j == 1 and i >= EARLY:
                     nc.scalar.copy(
                         out=pair[:, 0, 0 : UNIT // 2],
                         in_=right_of[i][:].rearrange("p e q t -> p (e q t)"),
@@ -222,7 +240,8 @@ def tile_gfsa_pa_kernel(tc, x, att, Wv, bv, w0, w1, wK, out):
                     func=COPY,
                     scale=c_att[:, h : h + 1],
                 )
-            regroup_right(nc.scalar.copy, i, 1, slice(0, SCALAR_PAIRS))
+            if i >= EARLY:
+                regroup_right(nc.scalar.copy, i, 1, slice(0, SCALAR_PAIRS))
 
         def add_identity(i):
             h = i % H
@@ -230,7 +249,7 @@ def tile_gfsa_pa_kernel(tc, x, att, Wv, bv, w0, w1, wK, out):
             nc.gpsimd.tensor_tensor(
                 out=diag, in0=diag, in1=eye[:, h, :].unsqueeze(1).to_broadcast([P, 3, P]), op=ADD
             )
-            last = scaled_of[i][:, 3 * DIAG_STEP : PACK * N]
+            last = scaled_of[i][:, 3 * DIAG_STEP : 3 * DIAG_STEP + P]
             nc.gpsimd.tensor_tensor(out=last, in0=last, in1=eye[:, h, :], op=ADD)
 
         def quantise_pair(i):
@@ -273,54 +292,53 @@ def tile_gfsa_pa_kernel(tc, x, att, Wv, bv, w0, w1, wK, out):
             head = slice(DH * h, DH * (h + 1))
             quantise(v_of[i][:].rearrange("p d t -> p (d t)"), v_codes[:, b, head], v_scales[:, b, head])
 
-        def filter_head(i, halfway):
+        def start_filter(i):
+            gf_of[i] = work_pool.tile([P, UNIT], BF16, name="gf_grouped", tag="gf_grouped", align_bytes=64)
+            gf_codes_of[i] = (
+                work_pool.tile([P, K_PASS], U32, name="g_codes", tag="g_codes", bufs=3, align_bytes=64),
+                work_pool.tile([P, K_PASS], U8, name="g_scales", tag="g_scales", bufs=3, align_bytes=64),
+            )
+
+        def filter_queries(i, c):
             h = i % H
             codes, scales = codes_of[i]
-            slabs = scaled_of[i][:].rearrange("p (t n) -> p t n", t=PACK)
-            gf_grouped = work_pool.tile([P, UNIT], BF16, tag="gf_grouped", align_bytes=64)
-            for c in range(N // P):
-                if c == 2:
-                    halfway()
-                queries = slice(P * c, P * (c + 1))
-                sq = mx_pool.tile([P, PACK, P], F32, tag="mx")
-                for t in range(PACK):
-                    keys = slice(P * t, P * (t + 1))
-                    mx(
-                        sq[:, t, :],
-                        codes[:, 0, keys],
-                        scales[:, 0, keys],
-                        codes[:, 1, queries],
-                        scales[:, 1, queries],
-                        True,
-                        True,
-                    )
-                nc.vector.scalar_tensor_tensor(
-                    out=gf_grouped[:, K_PASS * c : K_PASS * (c + 1)].rearrange(
-                        "p (n t) -> p n t", t=PACK
-                    ),
-                    in0=sq[:].rearrange("p t n -> p n t"),
-                    scalar=c_sq[:, h : h + 1],
-                    in1=slabs[:, :, queries].rearrange("p t n -> p n t"),
-                    op0=MULT,
-                    op1=ADD,
+            queries = slice(P * c, P * (c + 1))
+            sq = mx_pool.tile([P, PACK, P], F32, tag="mx")
+            for t in range(PACK):
+                keys = slice(P * t, P * (t + 1))
+                mx(
+                    sq[:, t, :],
+                    codes[:, 0, keys],
+                    scales[:, 0, keys],
+                    codes[:, 1, queries],
+                    scales[:, 1, queries],
+                    True,
+                    True,
                 )
-            gf_of[i] = gf_grouped
+            slabs = slabs_of(i)
+            nc.vector.scalar_tensor_tensor(
+                out=gf_of[i][:, K_PASS * c : K_PASS * (c + 1)].rearrange("p (n t) -> p n t", t=PACK),
+                in0=sq[:].rearrange("p t n -> p n t"),
+                scalar=c_sq[:, h : h + 1],
+                in1=slabs[:, :, queries].rearrange("p t n -> p n t"),
+                op0=MULT,
+                op1=ADD,
+            )
 
-        def quantise_gf(i):
-            g_codes = work_pool.tile([P, K_PASS], U32, tag="g_codes", bufs=3, align_bytes=64)
-            g_scales = work_pool.tile([P, K_PASS], U8, tag="g_scales", bufs=3, align_bytes=64)
-            quantise(gf_of[i][:], g_codes[:], g_scales[:])
-            gf_codes_of[i] = (g_codes, g_scales)
+        def quantise_gf(i, first, last):
+            g_codes, g_scales = gf_codes_of[i]
+            queries = slice(P * first, P * last)
+            quantise(gf_of[i][:, K_PASS * first : K_PASS * last], g_codes[:, queries], g_scales[:, queries])
 
-        def apply_head(i):
+        def apply_head(i, first, last, pool, tag):
             b, h = i // H, i % H
             head = slice(DH * h, DH * (h + 1))
             g_codes, g_scales = gf_codes_of[i]
-            o_acc = o_pool.tile([P, PACK, DH], F32, tag="o")
-            for t in range(PACK):
+            o_acc = pool.tile([P, last - first, DH], F32, name="o_acc", tag=tag)
+            for t in range(first, last):
                 queries = slice(P * t, P * (t + 1))
                 mx(
-                    o_acc[:, t, :],
+                    o_acc[:, t - first, :],
                     g_codes[:, queries],
                     g_scales[:, queries],
                     v_codes[:, b, head],
@@ -328,41 +346,49 @@ def tile_gfsa_pa_kernel(tc, x, att, Wv, bv, w0, w1, wK, out):
                     True,
                     True,
                 )
-            o_of[i] = o_acc
+            return o_acc
 
-        def store_head(i):
+        def store_head(i, first, last, o_acc):
             b, h = i // H, i % H
             head = slice(DH * h, DH * (h + 1))
-            o_sb = out_pool.tile([P, PACK, DH], F32, tag="o_sb")
-            nc.scalar.copy(out=o_sb[:], in_=o_of[i][:])
+            o_sb = out_pool.tile([P, last - first, DH], F32, name="o_sb", tag="o_sb")
+            nc.scalar.copy(out=o_sb[:], in_=o_acc[:])
             rows = out[b].rearrange(ROWS, u=2, e=2)
-            for u in range(2):
-                nc.sync.dma_start(out=rows[:, u, :, head], in_=o_sb[:, 2 * u : 2 * (u + 1), :])
+            for u in range(first // 2, last // 2):
+                slabs = slice(2 * u - first, 2 * u - first + 2)
+                nc.sync.dma_start(out=rows[:, u, :, head], in_=o_sb[:, slabs, :])
 
         def is_head(i):
             return 0 <= i < HEADS
 
-        for i in range(3):
-            start_pair(i)
+        def next_pair(i):
+            quantise_pair(i)
+            if is_head(i + 3):
+                start_pair(i + 3)
+            add_identity(i)
+
+        start_pair(0)
         transpose_att(0)
         unpack(0)
         for k in range(2 * D_PASSES):
             unpack_x(0, k, transpose_x(0, k, mx_pool, "mx"))
-        transpose_att(1)
         regroup_w(0)
         quantise_w(0)
+        start_pair(1)
+        start_pair(2)
+        transpose_att(1)
         quantise_pair(0)
-        start_pair(3)
         add_identity(0)
+        start_pair(3)
         unpack(1)
         transpose_att(2)
         regroup_w(1)
         quantise_w(1)
         quantise_x(0)
         x_bank = None
-        for step in range(2, HEADS + 6):
+        for step in range(2, HEADS + 1):
             if is_head(step - 5):
-                store_head(step - 5)
+                store_head(step - 5, 0, PACK, o_of[step - 5])
             if is_head(step):
                 unpack(step)
             if x_bank is not None:
@@ -370,15 +396,33 @@ def tile_gfsa_pa_kernel(tc, x, att, Wv, bv, w0, w1, wK, out):
             if step == 9:
                 quantise_x(1)
             if is_head(step - 4):
-                apply_head(step - 4)
-            if is_head(step - 1):
-                quantise_pair(step - 1)
-                if is_head(step + 2):
-                    start_pair(step + 2)
-                add_identity(step - 1)
-            if is_head(step - 2):
-                project(step - 2)
-                filter_head(step - 2, lambda: transpose_att(step + 1) if is_head(step + 1) else None)
-                x_bank = transpose_x(1, step - 4, tp_pool, "tp") if 4 <= step < 8 else None
-                quantise_v(step - 2)
-                quantise_gf(step - 2)
+                o_of[step - 4] = apply_head(step - 4, 0, PACK, o_pool, "o")
+            next_pair(step - 1)
+            start_filter(step - 2)
+            for c in range(PACK):
+                if c == PACK - 1 and is_head(step + 1):
+                    transpose_att(step + 1)
+                filter_queries(step - 2, c)
+            project(step - 2)
+            x_bank = transpose_x(1, step - 4, tp_pool, "tp") if 4 <= step < 8 else None
+            quantise_gf(step - 2, 0, PACK)
+            quantise_v(step - 2)
+        i = HEADS - 1
+        store_head(i - 3, 0, PACK, o_of[i - 3])
+        o_of[i - 2] = apply_head(i - 2, 0, PACK, o_pool, "o")
+        store_head(i - 2, 0, PACK, o_of[i - 2])
+        project(i)
+        start_filter(i)
+        for c in range(PACK // 2):
+            filter_queries(i, c)
+        quantise_v(i)
+        o_of[i - 1] = apply_head(i - 1, 0, PACK, o_pool, "o")
+        store_head(i - 1, 0, PACK, o_of[i - 1])
+        quantise_gf(i, 0, PACK // 2)
+        for c in range(PACK // 2, PACK):
+            filter_queries(i, c)
+        o_half = apply_head(i, 0, PACK // 2, mx_pool, "mx")
+        store_head(i, 0, PACK // 2, o_half)
+        quantise_gf(i, PACK // 2, PACK)
+        o_half = apply_head(i, PACK // 2, PACK, mx_pool, "mx")
+        store_head(i, PACK // 2, PACK, o_half)

from contextlib import ExitStack

import concourse.mybir as mybir
from concourse.masks import make_identity

BF16 = mybir.dt.bfloat16
F32 = mybir.dt.float32
U32 = mybir.dt.uint32
U8 = mybir.dt.uint8
FP8X4 = mybir.dt.float8_e4m3fn_x4
MULT = mybir.AluOpType.mult
ADD = mybir.AluOpType.add
SUBTRACT = mybir.AluOpType.subtract
COPY = mybir.ActivationFunctionType.Copy

P = 128
PACK = 4
K_PASS = P * PACK
B, N, D, H, DH = 2, 512, 1024, 8, 128
HEADS = B * H
D_PASSES = D // K_PASS
UNIT = K_PASS * PACK
EARLY = 1
SCALAR_PAIRS = 64

FLOPS = 2 * B * N * D * D + HEADS * 2 * N * N * N + HEADS * 2 * N * N * DH

SLAB_STEP = N + 4
DIAG_STEP = SLAB_STEP + P

ROWS = "(u q e) c -> q u e c"
SLABS = "p (u e) c -> p u e c"
FROM = "p t (c i) -> p c t i"
INTO = "p (c i t) -> p c t i"


def tile_gfsa_pa_kernel(tc, x, att, Wv, bv, w0, w1, wK, out):
    nc = tc.nc
    with ExitStack() as ctx:
        resident = ctx.enter_context(tc.tile_pool(name="resident", bufs=1))
        wide_pool = ctx.enter_context(tc.tile_pool(name="wide", bufs=2))
        pair_pool = ctx.enter_context(tc.tile_pool(name="pair", bufs=3))
        scaled_pool = ctx.enter_context(tc.tile_pool(name="scaled", bufs=4))
        work_pool = ctx.enter_context(tc.tile_pool(name="work", bufs=2))
        out_pool = ctx.enter_context(tc.tile_pool(name="outs", bufs=3))
        tp_pool = ctx.enter_context(tc.psum_pool(name="tp", bufs=3))
        right_pool = ctx.enter_context(tc.psum_pool(name="right", bufs=1))
        mx_pool = ctx.enter_context(tc.psum_pool(name="mx", bufs=3))
        o_pool = ctx.enter_context(tc.psum_pool(name="o", bufs=1))
        ctx.enter_context(tc.manual_schedule())

        ident = resident.tile([P, P], F32)
        make_identity(nc, ident[:])
        ident_bf = resident.tile([P, P], BF16)
        nc.gpsimd.tensor_copy(out=ident_bf[:], in_=ident[:])

        w0_bf = resident.tile([P, H], BF16)
        w1_bf = resident.tile([P, H], BF16)
        wk_bf = resident.tile([P, H], BF16)
        nc.sync.dma_start(out=w1_bf[:], in_=w1.partition_broadcast(P))
        nc.sync.dma_start(out=wk_bf[:], in_=wK.partition_broadcast(P))
        nc.sync.dma_start(out=w0_bf[:], in_=w0.partition_broadcast(P))

        x_sb = [resident.tile([P, PACK, D], BF16, name="x_sb%d" % b) for b in range(B)]
        w_sb = resident.tile([P, D_PASSES, PACK, D], BF16)
        att_sb = [resident.tile([P, PACK, N], BF16, name="att_sb%d" % i) for i in range(HEADS)]
        bias = resident.tile([P, D], BF16)

        def load_att(i):
            nc.sync.dma_start(
                out=att_sb[i][:].rearrange(SLABS, u=2),
                in_=att[i // H, i % H].rearrange(ROWS, u=2, e=2),
            )

        def load_x(b):
            nc.sync.dma_start(out=x_sb[b][:].rearrange(SLABS, u=2), in_=x[b].rearrange(ROWS, u=2, e=2))

        def load_w(g):
            nc.sync.dma_start(
                out=w_sb[:, g].rearrange(SLABS, u=2),
                in_=Wv[K_PASS * g : K_PASS * (g + 1), :].rearrange(ROWS, u=2, e=2),
            )

        load_att(0)
        load_w(0)
        load_x(0)
        load_att(1)
        load_w(1)
        load_att(2)
        nc.sync.dma_start(out=bias[:], in_=bv.partition_broadcast(P))
        load_att(3)
        load_x(1)
        load_att(4)
        load_att(5)
        load_att(6)
        load_att(7)
        load_att(8)
        load_att(9)
        load_att(10)
        load_att(11)
        load_att(12)
        load_att(13)
        load_att(14)
        load_att(15)

        c_eye = resident.tile([P, H], F32)
        c_att = resident.tile([P, H], F32)
        c_sq = resident.tile([P, H], F32)
        nc.vector.tensor_tensor(out=c_att[:], in0=w1_bf[:], in1=wk_bf[:], op=SUBTRACT)
        nc.vector.tensor_scalar(out=c_sq[:], in0=wk_bf[:], scalar1=2.0, scalar2=None, op0=MULT)
        nc.gpsimd.tensor_copy(out=c_eye[:], in_=w0_bf[:])
        eye = resident.tile([P, H, P], BF16)
        for h in range(H):
            nc.gpsimd.tensor_scalar(
                out=eye[:, h, :], in0=ident[:], scalar1=c_eye[:, h : h + 1], scalar2=0.0, op0=MULT, op1=ADD
            )

        x_codes = resident.tile([P, B, D_PASSES * K_PASS], U32, align_bytes=64)
        x_scales = resident.tile([P, B, D_PASSES * K_PASS], U8, align_bytes=64)
        w_codes = resident.tile([P, D_PASSES, D], U32, align_bytes=64)
        w_scales = resident.tile([P, D_PASSES, D], U8, align_bytes=64)
        v_codes = resident.tile([P, B, D], U32, align_bytes=64)
        v_scales = resident.tile([P, B, D], U8, align_bytes=64)

        def quantise(grouped, codes, scales):
            nc.vector.quantize_mx(out=codes.bitcast(FP8X4), scales=scales, in_=grouped)

        def transpose_bank(src, j, pool, tag):
            bank = pool.tile([P, 2, 2 * P], F32, name="bank", tag=tag)
            for u in range(2):
                for s in range(2):
                    words = src[:, 2 * j + s, :].bitcast(F32)
                    nc.tensor.transpose(
                        bank[:, u, P * s : P * (s + 1)], words[:, P * u : P * (u + 1)], ident[:]
                    )
            return bank

        def pack_bank(copy, bank, j, grouped):
            copy(
                out=grouped.bitcast(F32)[:, K_PASS * j : K_PASS * (j + 1)].rearrange("p (c u) -> p c u", u=2),
                in_=bank[:].rearrange("p u c -> p c u"),
            )

        def mx(acc, lhs_codes, lhs_scales, rhs_codes, rhs_scales, start, stop):
            nc.tensor.matmul_mx(
                out=acc,
                lhsT=lhs_codes.bitcast(FP8X4),
                lhsT_scale=lhs_scales,
                rhs=rhs_codes.bitcast(FP8X4),
                rhs_scale=rhs_scales,
                start=start,
                stop=stop,
            )

        def transpose_x(b, k, pool, tag):
            g, j = divmod(k, 2)
            return transpose_bank(x_sb[b][:, :, K_PASS * g : K_PASS * (g + 1)], j, pool, tag)

        def unpack_x(b, k, bank):
            g, j = divmod(k, 2)
            if k == 0:
                x_wide_of[b] = wide_pool.tile(
                    [P, D_PASSES, UNIT], BF16, name="x_wide", tag="wide", align_bytes=64
                )
            pack_bank(nc.scalar.copy, bank, j, x_wide_of[b][:, g, :])

        def quantise_x(b):
            quantise(x_wide_of[b][:].rearrange("p g c -> p (g c)"), x_codes[:, b, :], x_scales[:, b, :])

        def regroup_w(g):
            w_wide_of[g] = wide_pool.tile([P, 2 * UNIT], BF16, name="w_wide", tag="wide", align_bytes=64)
            nc.vector.tensor_copy(
                out=w_wide_of[g][:].rearrange(INTO, i=4, t=PACK), in_=w_sb[:, g].rearrange(FROM, i=4)
            )

        def quantise_w(g):
            quantise(w_wide_of[g][:], w_codes[:, g, :], w_scales[:, g, :])

        x_wide_of = [None] * B
        w_wide_of = [None] * D_PASSES
        banks_of = [None] * HEADS
        right_of = [None] * HEADS
        pair_of = [None] * HEADS
        scaled_of = [None] * HEADS
        codes_of = [None] * HEADS
        gf_of = [None] * HEADS
        v_of = [None] * HEADS
        o_of = [None] * HEADS
        gf_codes_of = [None] * HEADS

        def transpose_att(i):
            banks_of[i] = [transpose_bank(att_sb[i], j, tp_pool, "tp") for j in range(2)]
            if i < EARLY:
                return
            bank = right_pool.tile([P, 2, P, PACK], BF16, tag="right")
            for t in range(0, PACK, 2):
                nc.tensor.matmul(
                    bank[:, :, :, t : t + 2],
                    lhsT=ident_bf[:],
                    rhs=att_sb[i][:, t : t + 2, 0 : 2 * P].rearrange("p t (q e) -> p e q t", e=2),
                    start=True,
                    stop=True,
                )
            right_of[i] = bank

        def regroup_right(copy, i, u, pairs):
            tiles = pair_of[i][:, 0, :].rearrange("p (u e q t) -> p u q e t", u=2, e=2, t=PACK)
            keys = att_sb[i][:].rearrange("p t (u q e) -> p u q e t", u=2, e=2)
            copy(out=tiles[:, u, pairs], in_=keys[:, u, pairs])

        def gpsimd_copy(out, in_):
            nc.gpsimd.tensor_scalar(out=out, in0=in_, scalar1=1.0, scalar2=0.0, op0=MULT, op1=ADD)

        def start_pair(i):
            pair_of[i] = pair_pool.tile([P, 2, UNIT], BF16, name="pair", tag="pair", align_bytes=64)
            if i >= EARLY:
                regroup_right(gpsimd_copy, i, 1, slice(SCALAR_PAIRS, P))
            else:
                for u in range(2):
                    regroup_right(nc.vector.tensor_copy, i, u, slice(0, P))

        def slabs_of(i):
            return scaled_of[i][:].rearrange("p (t n) -> p t n", t=PACK)[:, :, 0:N]

        def unpack(i):
            h = i % H
            pair = pair_of[i]
            scaled_of[i] = scaled_pool.tile([P, PACK * SLAB_STEP], F32, name="scaled", tag="scaled")
            slabs = slabs_of(i)
            for j in range(2):
                if j == 1 and i >= EARLY:
                    nc.scalar.copy(
                        out=pair[:, 0, 0 : UNIT // 2],
                        in_=right_of[i][:].rearrange("p e q t -> p (e q t)"),
                    )
                pack_bank(nc.scalar.copy, banks_of[i][j], j, pair[:, 1, :])
                nc.scalar.activation(
                    out=slabs[:, :, 2 * P * j : 2 * P * (j + 1)].rearrange(SLABS, u=2),
                    in_=banks_of[i][j][:].bitcast(BF16).rearrange("p u (c e) -> p u e c", e=2),
                    func=COPY,
                    scale=c_att[:, h : h + 1],
                )
            if i >= EARLY:
                regroup_right(nc.scalar.copy, i, 1, slice(0, SCALAR_PAIRS))

        def add_identity(i):
            h = i % H
            diag = scaled_of[i][:, 0 : 3 * DIAG_STEP].rearrange("p (t w) -> p t w", w=DIAG_STEP)[:, :, 0:P]
            nc.gpsimd.tensor_tensor(
                out=diag, in0=diag, in1=eye[:, h, :].unsqueeze(1).to_broadcast([P, 3, P]), op=ADD
            )
            last = scaled_of[i][:, 3 * DIAG_STEP : 3 * DIAG_STEP + P]
            nc.gpsimd.tensor_tensor(out=last, in0=last, in1=eye[:, h, :], op=ADD)

        def quantise_pair(i):
            codes = work_pool.tile([P, 2, K_PASS], U32, tag="codes", align_bytes=64)
            scales = work_pool.tile([P, 2, K_PASS], U8, tag="scales", align_bytes=64)
            quantise(
                pair_of[i][:].rearrange("p a c -> p (a c)"),
                codes[:].rearrange("p a c -> p (a c)"),
                scales[:].rearrange("p a c -> p (a c)"),
            )
            codes_of[i] = (codes, scales)

        def project(i):
            b, h = i // H, i % H
            head = slice(DH * h, DH * (h + 1))
            v_acc = mx_pool.tile([P, PACK, DH], F32, tag="mx")
            for t in range(PACK):
                for g in range(D_PASSES):
                    tokens = slice(K_PASS * g + P * t, K_PASS * g + P * (t + 1))
                    mx(
                        v_acc[:, t, :],
                        x_codes[:, b, tokens],
                        x_scales[:, b, tokens],
                        w_codes[:, g, head],
                        w_scales[:, g, head],
                        g == 0,
                        g == D_PASSES - 1,
                    )
            v_grouped = work_pool.tile([P, DH, PACK], BF16, tag="v_grouped", align_bytes=64)
            nc.vector.tensor_tensor(
                out=v_grouped[:],
                in0=v_acc[:].rearrange("p t d -> p d t"),
                in1=bias[:, head].unsqueeze(2).to_broadcast([P, DH, PACK]),
                op=ADD,
            )
            v_of[i] = v_grouped

        def quantise_v(i):
            b, h = i // H, i % H
            head = slice(DH * h, DH * (h + 1))
            quantise(v_of[i][:].rearrange("p d t -> p (d t)"), v_codes[:, b, head], v_scales[:, b, head])

        def start_filter(i):
            gf_of[i] = work_pool.tile([P, UNIT], BF16, name="gf_grouped", tag="gf_grouped", align_bytes=64)
            gf_codes_of[i] = (
                work_pool.tile([P, K_PASS], U32, name="g_codes", tag="g_codes", bufs=3, align_bytes=64),
                work_pool.tile([P, K_PASS], U8, name="g_scales", tag="g_scales", bufs=3, align_bytes=64),
            )

        def filter_queries(i, c):
            h = i % H
            codes, scales = codes_of[i]
            queries = slice(P * c, P * (c + 1))
            sq = mx_pool.tile([P, PACK, P], F32, tag="mx")
            for t in range(PACK):
                keys = slice(P * t, P * (t + 1))
                mx(
                    sq[:, t, :],
                    codes[:, 0, keys],
                    scales[:, 0, keys],
                    codes[:, 1, queries],
                    scales[:, 1, queries],
                    True,
                    True,
                )
            slabs = slabs_of(i)
            nc.vector.scalar_tensor_tensor(
                out=gf_of[i][:, K_PASS * c : K_PASS * (c + 1)].rearrange("p (n t) -> p n t", t=PACK),
                in0=sq[:].rearrange("p t n -> p n t"),
                scalar=c_sq[:, h : h + 1],
                in1=slabs[:, :, queries].rearrange("p t n -> p n t"),
                op0=MULT,
                op1=ADD,
            )

        def quantise_gf(i, first, last):
            g_codes, g_scales = gf_codes_of[i]
            queries = slice(P * first, P * last)
            quantise(gf_of[i][:, K_PASS * first : K_PASS * last], g_codes[:, queries], g_scales[:, queries])

        def apply_head(i, first, last, pool, tag):
            b, h = i // H, i % H
            head = slice(DH * h, DH * (h + 1))
            g_codes, g_scales = gf_codes_of[i]
            o_acc = pool.tile([P, last - first, DH], F32, name="o_acc", tag=tag)
            for t in range(first, last):
                queries = slice(P * t, P * (t + 1))
                mx(
                    o_acc[:, t - first, :],
                    g_codes[:, queries],
                    g_scales[:, queries],
                    v_codes[:, b, head],
                    v_scales[:, b, head],
                    True,
                    True,
                )
            return o_acc

        def store_head(i, first, last, o_acc):
            b, h = i // H, i % H
            head = slice(DH * h, DH * (h + 1))
            o_sb = out_pool.tile([P, last - first, DH], F32, name="o_sb", tag="o_sb")
            nc.scalar.copy(out=o_sb[:], in_=o_acc[:])
            rows = out[b].rearrange(ROWS, u=2, e=2)
            for u in range(first // 2, last // 2):
                slabs = slice(2 * u - first, 2 * u - first + 2)
                nc.sync.dma_start(out=rows[:, u, :, head], in_=o_sb[:, slabs, :])

        def is_head(i):
            return 0 <= i < HEADS

        def next_pair(i):
            quantise_pair(i)
            if is_head(i + 3):
                start_pair(i + 3)
            add_identity(i)

        start_pair(0)
        transpose_att(0)
        unpack(0)
        for k in range(2 * D_PASSES):
            unpack_x(0, k, transpose_x(0, k, mx_pool, "mx"))
        regroup_w(0)
        quantise_w(0)
        start_pair(1)
        start_pair(2)
        transpose_att(1)
        quantise_pair(0)
        add_identity(0)
        start_pair(3)
        unpack(1)
        transpose_att(2)
        regroup_w(1)
        quantise_w(1)
        quantise_x(0)
        x_bank = None
        for step in range(2, HEADS + 1):
            if is_head(step - 5):
                store_head(step - 5, 0, PACK, o_of[step - 5])
            if is_head(step):
                unpack(step)
            if x_bank is not None:
                unpack_x(1, step - 5, x_bank)
            if step == 9:
                quantise_x(1)
            if is_head(step - 4):
                o_of[step - 4] = apply_head(step - 4, 0, PACK, o_pool, "o")
            next_pair(step - 1)
            start_filter(step - 2)
            for c in range(PACK):
                if c == PACK - 1 and is_head(step + 1):
                    transpose_att(step + 1)
                filter_queries(step - 2, c)
            project(step - 2)
            x_bank = transpose_x(1, step - 4, tp_pool, "tp") if 4 <= step < 8 else None
            quantise_gf(step - 2, 0, PACK)
            quantise_v(step - 2)
        i = HEADS - 1
        store_head(i - 3, 0, PACK, o_of[i - 3])
        o_of[i - 2] = apply_head(i - 2, 0, PACK, o_pool, "o")
        store_head(i - 2, 0, PACK, o_of[i - 2])
        project(i)
        start_filter(i)
        for c in range(PACK // 2):
            filter_queries(i, c)
        quantise_v(i)
        o_of[i - 1] = apply_head(i - 1, 0, PACK, o_pool, "o")
        store_head(i - 1, 0, PACK, o_of[i - 1])
        quantise_gf(i, 0, PACK // 2)
        for c in range(PACK // 2, PACK):
            filter_queries(i, c)
        o_half = apply_head(i, 0, PACK // 2, mx_pool, "mx")
        store_head(i, 0, PACK // 2, o_half)
        quantise_gf(i, PACK // 2, PACK)
        o_half = apply_head(i, PACK // 2, PACK, mx_pool, "mx")
        store_head(i, PACK // 2, PACK, o_half)
